import numpy as np
import ml_dtypes


def mxq(x, axis, fmt="e4m3"):
    dtype, down = {"e4m3": (ml_dtypes.float8_e4m3fn, 7), "e5m2": (ml_dtypes.float8_e5m2, 14)}[fmt]
    v = np.moveaxis(np.asarray(x, np.float32).astype(ml_dtypes.bfloat16).astype(np.float64), axis, -1)
    blocks = v.reshape(v.shape[:-1] + (-1, 32))
    amax = np.abs(blocks).max(-1, keepdims=True)
    byte = np.maximum(np.where(amax > 0, np.frexp(amax)[1] - 1 + 127, 0) - down, 1)
    scale = np.exp2(byte - 127.0)
    codes = (blocks / scale).astype(np.float32).astype(dtype).astype(np.float64)
    return np.moveaxis((codes * scale).reshape(v.shape), -1, axis)


WIDE = False


def mx_kscale(k):
    if not WIDE:
        return np.ones(k)
    levels = np.array([10, -10, 5, -5, 0])
    if k % 512:
        return np.exp2(np.random.permutation(np.resize(levels, k // 32))).repeat(32)
    a = np.empty((k // 512, 16))
    for p in range(k // 512):
        a[p, :8] = np.random.permutation(np.resize(levels, 8))
        for g in range(8):
            far = levels[np.abs(levels - a[p, g]) >= 10]
            a[p, g + 8] = far[np.random.randint(len(far))]
    return np.exp2(a.ravel()).repeat(32)


BF16 = ml_dtypes.bfloat16


def bf(x):
    return np.asarray(x, np.float32).astype(BF16)


def f64(x):
    return np.asarray(x).astype(np.float64)


B, C, H, W, ATT_DEPTH, PATCH = 1, 8, 512, 512, 1, 8
DS = 2 ** ATT_DEPTH
HS, WS = H // (PATCH * DS), W // (PATCH * DS)
HT, WT = H // PATCH, W // PATCH
LP, L, N = HS * WS, HT * WT, C * PATCH * PATCH


def setup_inputs():
    s = mx_kscale(LP)
    sx = np.repeat(np.repeat(s.reshape(HS, WS), PATCH * DS, axis=0), PATCH * DS, axis=1)
    x = np.random.standard_normal((B, C, H, W)) * 2.0 * DS / sx
    keep = 0.25 + 0.75 * np.random.random((B, 1, L, 1))
    keep = keep * (np.random.random((B, 1, L, 1)) >= 0.03)
    a = np.random.random((B, 1, L, LP)) * (np.random.random((B, 1, L, LP)) < keep)
    return {"x": bf(x), "attentions": bf(a * 0.3 * np.sqrt(LP) * s)}


def reference(x, attentions):
    x, attentions = f64(x), f64(attentions)
    argx = x.reshape(B, C, H // DS, DS, W // DS, DS).mean(axis=(3, 5))
    unf = argx.reshape(B, C, HS, PATCH, WS, PATCH).transpose(0, 1, 3, 5, 2, 4).reshape(B, N, LP)
    nz = np.where(attentions != 0.0, 1.0, 0.0).sum(axis=-1, keepdims=True) + 1e-05
    a = attentions / nz
    att = mxq(a, 3, "e4m3") @ mxq(unf[:, None].transpose(0, 1, 3, 2), 2, "e4m3")
    att = att[:, 0].transpose(0, 2, 1)
    return att.reshape(B, C, PATCH, PATCH, HT, WT).transpose(0, 1, 4, 2, 5, 3).reshape(B, C, H, W)

@@ -1,0 +1,289 @@
+from contextlib import ExitStack
+
+import concourse.mybir as mybir
+from concourse.masks import make_identity
+
+BF16 = mybir.dt.bfloat16
+F32 = mybir.dt.float32
+U32 = mybir.dt.uint32
+U8 = mybir.dt.uint8
+FP8X4 = mybir.dt.float8_e4m3fn_x4
+ALU = mybir.AluOpType
+ACT = mybir.ActivationFunctionType
+
+P = 128
+L = 4096
+LP = 1024
+N = 512
+FLOPS = 2 * L * LP * N
+
+NH = 2
+G = L // (P * NH)
+NB = 64 // G
+RC = 4
+NT = L // P
+NP = NT // 2
+PIN = True
+LM = 4
+M0 = 8
+CR = 3
+UQ = 8
+PX = [0,2,4,5]
+
+
+def tile_decode_atten_t_kernel(tc, x, attentions, out):
+    nc = tc.nc
+    with ExitStack() as ctx:
+        if PIN:
+            ctx.enter_context(tc.manual_schedule())
+        const = ctx.enter_context(tc.tile_pool(name="const", bufs=1))
+        xpool = ctx.enter_context(tc.tile_pool(name="xpool", bufs=4))
+        gpool = ctx.enter_context(tc.tile_pool(name="gpool", bufs=2))
+        apool = ctx.enter_context(tc.tile_pool(name="apool", bufs=6))
+        work = ctx.enter_context(tc.tile_pool(name="work", bufs=4))
+        jpool = ctx.enter_context(tc.tile_pool(name="jpool", bufs=2))
+        small = ctx.enter_context(tc.tile_pool(name="small", bufs=4))
+        rpool = ctx.enter_context(tc.tile_pool(name="rpool", bufs=3))
+        qpool = ctx.enter_context(tc.tile_pool(name="qpool", bufs=8))
+        opool = ctx.enter_context(tc.tile_pool(name="opool", bufs=2))
+        psum_t = ctx.enter_context(tc.psum_pool(name="psum_t", bufs=4))
+        psum_o = ctx.enter_context(tc.psum_pool(name="psum_o", bufs=4))
+
+        ident = const.tile([P, P], BF16)
+        make_identity(nc, ident[:])
+        uq = const.tile([P, 2, N, 4], BF16, align_bytes=64)
+        ucodes = const.tile([P, 2, N], U32, align_bytes=64)
+        uscales = const.tile([P, 2, N], U8, align_bytes=64)
+
+        xv = x[0].rearrange("c (s jl kh d) w -> jl (c s) kh (d w)", s=2, jl=16, kh=8, d=2)
+        attv = attentions[0, 0].rearrange("(h p r) j -> h p r j", h=NH, p=P, r=G)
+        ov = out[0].rearrange("c (h lh kh) (b w) -> c h b lh kh w", h=NH, kh=8, b=NB)
+
+        xs = {}
+        chunks = {}
+
+        def load_x(k):
+            xs_k = xpool.tile([P, 4, 2, 512], BF16, name="xs")
+            for a in range(4):
+                nc.sync.dma_start(
+                    out=xs_k[:, a].rearrange("p d w -> p (d w)"), in_=xv[4 * k + a]
+                )
+            xs[k] = xs_k
+
+        def load_att(ci):
+            at_c = apool.tile([P, RC, LP], BF16, name="at_c")
+            h, r0 = divmod(ci * RC, G)
+            nc.sync.dma_start(out=at_c[:], in_=attv[h, :, r0 : r0 + RC, :])
+            chunks[ci] = at_c
+
+        for item in [["x",0],["a",0],["x",1],["a",1],["x",2],["x",3],["a",2],["a",3],["a",4],["a",5],["a",6],["a",7]]:
+            if item[0] == "x":
+                load_x(item[1])
+            else:
+                load_att(item[1])
+
+        def row(t):
+            return chunks[t // RC][:, t % RC, :]
+
+        state = {}
+
+        g = const.tile([P, 16 * 256], BF16)
+
+        def pool_vector(k):
+            s1 = const.tile([P, 4, 512], F32, name="s1")
+            nc.vector.tensor_tensor(out=s1[:], in0=xs[k][:, :, 0, :], in1=xs[k][:, :, 1, :], op=ALU.add)
+            s1v = s1[:].rearrange("p a (m d) -> p (a m) d", d=2)
+            nc.vector.tensor_tensor(
+                out=g[:, k * 1024 : (k + 1) * 1024], in0=s1v[:, :, 0], in1=s1v[:, :, 1], op=ALU.add
+            )
+
+        def pool_matmuls(k):
+            banks = []
+            for beta in range(2):
+                ps = psum_o.tile([P, 512], F32, name="mo")
+                for d in range(2):
+                    cols = xs[k][:, 2 * beta : 2 * beta + 2, d, :].rearrange("p a (m e) -> p a m e", e=2)
+                    for e in range(2):
+                        nc.tensor.matmul(
+                            out=ps[:],
+                            lhsT=ident[:],
+                            rhs=cols[:, :, :, e],
+                            start=(d == 0 and e == 0),
+                            stop=(d == 1 and e == 1),
+                        )
+                banks.append(ps)
+            state[("ps", k)] = banks
+
+        def round_g(k):
+            for beta in range(2):
+                c0 = (2 * k + beta) * 512
+                nc.scalar.copy(out=g[:, c0 : c0 + 512], in_=state[("ps", k)][beta][:])
+
+        def transpose_u(b):
+            tp = psum_o.tile([P, 1024], BF16, name="mo")
+            for kk in range(2):
+                for t in range(4):
+                    o = (4 * kk + t) * P
+                    nc.tensor.transpose(tp[:, o : o + P], g[:, t * 8 + 2 * b + kk :: 32], ident[:])
+            state[("tu", b)] = tp
+
+        def regroup_u(b):
+            tv = state[("tu", b)][:].rearrange("p (q c s h) -> p s c h q", q=8, c=8, s=2, h=8)
+            for s in range(2):
+                dst = uq[:, s].rearrange("p (c h b2 kk) t -> p b2 c h (kk t)", c=8, h=8, b2=4, kk=2)
+                nc.scalar.copy(out=dst[:, b], in_=tv[:, s])
+
+        def quantise_u():
+            for s in range(2):
+                nc.vector.quantize_mx(
+                    out=ucodes[:, s, :].bitcast(FP8X4),
+                    scales=uscales[:, s, :],
+                    in_=uq[:, s].rearrange("p n t -> p (n t)"),
+                )
+
+        def count(i):
+            nz = small.tile([P, 2], F32, name="nz")
+            for j in range(2):
+                junk = jpool.tile([P, LP], BF16, name="junk")
+                nc.vector.tensor_scalar(
+                    out=junk[:],
+                    in0=row(2 * i + j),
+                    scalar1=0.0,
+                    scalar2=1e-05,
+                    op0=ALU.not_equal,
+                    op1=ALU.add,
+                    accum_out=nz[:, j : j + 1],
+                )
+            rnz = small.tile([P, 2], F32, name="rnz")
+            nc.vector.reciprocal(out=rnz[:], in_=nz[:])
+            state[("rnz", i)] = rnz
+
+        def scale(i):
+            rnz = state[("rnz", i)]
+            tiles = []
+            for j in range(2):
+                a_t = work.tile([P, LP], BF16, name="a_t")
+                nc.vector.tensor_scalar(
+                    out=a_t[:], in0=row(2 * i + j), scalar1=rnz[:, j : j + 1], scalar2=None, op0=ALU.mult
+                )
+                tiles.append(a_t)
+            state[("a", i)] = tiles
+
+        def transpose(i):
+            banks = []
+            for j in range(2):
+                a_t = state[("a", i)][j]
+                tp = psum_t.tile([P, 1024], BF16, name="tp")
+                for b in range(8):
+                    nc.tensor.transpose(
+                        tp[:, b * P : (b + 1) * P], a_t[:, (b // 4) * 512 + b % 4 : (b // 4 + 1) * 512 : 4], ident[:]
+                    )
+                banks.append(tp)
+            state[("tp", i)] = banks
+
+        def regroup(i):
+            grp = rpool.tile([P, 2, 2, P, 4], BF16, name="grp", align_bytes=64)
+            for j in range(2):
+                nc.scalar.copy(
+                    out=grp[:, j], in_=state[("tp", i)][j][:].rearrange("p (s t l) -> p s l t", s=2, t=4)
+                )
+            state[("grp", i)] = grp
+
+        def quantise(i):
+            codes = qpool.tile([P, 4 * P], U32, name="codes", align_bytes=64)
+            scl = qpool.tile([P, 4 * P], U8, name="scl", align_bytes=64)
+            nc.vector.quantize_mx(
+                out=codes[:].bitcast(FP8X4),
+                scales=scl[:],
+                in_=state[("grp", i)][:].rearrange("p j s l t -> p (j s l t)"),
+            )
+            state[("q", i)] = (codes, scl)
+        def multiply(i):
+            codes, scl = state[("q", i)]
+            banks = []
+            for j in range(2):
+                mo = psum_o.tile([P, N], F32, name="mo")
+                for s in range(2):
+                    c0 = (2 * j + s) * P
+                    nc.tensor.matmul_mx(
+                        out=mo[:],
+                        lhsT=codes[:, c0 : c0 + P].bitcast(FP8X4),
+                        lhsT_scale=scl[:, c0 : c0 + P],
+                        rhs=ucodes[:, s, :].bitcast(FP8X4),
+                        rhs_scale=uscales[:, s, :],
+                        start=(s == 0),
+                        stop=(s == 1),
+                    )
+                banks.append(mo)
+            state[("mo", i)] = banks
+
+
+        def store(h, stage, r0, r1):
+            for c in range(8):
+                for b in range(NB):
+                    nc.sync.dma_start(
+                        out=ov[c, h, b][:, :, r0 * 8 : r1 * 8],
+                        in_=stage[b:P:NB, c * 8 : (c + 1) * 8, r0:r1, :].rearrange("p kh r w -> p kh (r w)"),
+                    )
+
+        def on_vector(t):
+            return t % 2 == 1
+
+        def empty(i, vector):
+            for j in range(2):
+                t = 2 * i + j
+                h, r = divmod(t, G)
+                if ("stage", h) not in state:
+                    state[("stage", h)] = opool.tile([P, 64, G, 8], F32, name="stage")
+                stage = state[("stage", h)]
+                dst = stage[:, :, r, :]
+                src = state[("mo", i)][j][:].rearrange("p (m w) -> p m w", w=8)
+                if vector and on_vector(t):
+                    nc.vector.tensor_scalar(out=dst, in0=src, scalar1=0.25, scalar2=None, op0=ALU.mult)
+                if not vector and not on_vector(t):
+                    nc.scalar.activation(out=dst, in_=src, func=ACT.Copy, scale=0.25)
+
+        def stores_after(i):
+            h, r = divmod(2 * i + 1, G)
+            stage = state[("stage", h)]
+            if r == G // 2 - 1:
+                store(h, stage, 0, G // 2)
+            if r == G - 1:
+                store(h, stage, G // 2, G)
+
+        def m_step(i):
+            return max(i + LM, M0 + (i + CR - 1) // CR)
+
+        pool_vector(0)
+        for n in range(NP + LM + 1):
+            due = [i for i in range(NP) if m_step(i) == n]
+            if n == UQ:
+                quantise_u()
+            for i in due:
+                multiply(i)
+            for k in range(1, 4):
+                if PX[k] == n:
+                    pool_matmuls(k)
+            if n == PX[3] + 1:
+                for b in range(4):
+                    transpose_u(b)
+            if 0 <= n - 1 < NP:
+                transpose(n - 1)
+            for i in due:
+                empty(i, True)
+            if n < NP:
+                count(n)
+                scale(n)
+            if 0 <= n - 2 < NP:
+                quantise(n - 2)
+            if n == PX[3] + 1:
+                for b in range(4):
+                    regroup_u(b)
+            for i in due:
+                empty(i, False)
+                stores_after(i)
+            for k in range(1, 4):
+                if PX[k] == n:
+                    round_g(k)
+            if 0 <= n - 1 < NP:
+                regroup(n - 1)

@@ -17,29 +17,25 @@ LP = 1024
 N = 512
 FLOPS = 2 * L * LP * N
 
-NH = 2
-G = L // (P * NH)
-NB = 64 // G
-RC = 4
 NT = L // P
 NP = NT // 2
-PIN = True
-LM = 4
-M0 = 8
-CR = 3
-UQ = 8
-PX = [0,2,4,5]
+HALF = NT // 2
+CHUNKS = [2, 2, 4, 4, 4, 4, 4, 4, 4]
+LOADS = ["a", "x", "a", "x", "x", "a", "x", "a", "a", "a", "a", "a", "a"]
+PX = [0, 1, 2, 4]
+TU = 5
+UQ = 6
+M0 = 6
+LM = 3
 
 
 def tile_decode_atten_t_kernel(tc, x, attentions, out):
     nc = tc.nc
     with ExitStack() as ctx:
-        if PIN:
-            ctx.enter_context(tc.manual_schedule())
+        ctx.enter_context(tc.manual_schedule())
         const = ctx.enter_context(tc.tile_pool(name="const", bufs=1))
         xpool = ctx.enter_context(tc.tile_pool(name="xpool", bufs=4))
-        gpool = ctx.enter_context(tc.tile_pool(name="gpool", bufs=2))
-        apool = ctx.enter_context(tc.tile_pool(name="apool", bufs=6))
+        apool = ctx.enter_context(tc.tile_pool(name="apool", bufs=7))
         work = ctx.enter_context(tc.tile_pool(name="work", bufs=4))
         jpool = ctx.enter_context(tc.tile_pool(name="jpool", bufs=2))
         small = ctx.enter_context(tc.tile_pool(name="small", bufs=4))
@@ -51,51 +47,54 @@ def tile_decode_atten_t_kernel(tc, x, attentions, out):
 
         ident = const.tile([P, P], BF16)
         make_identity(nc, ident[:])
-        uq = const.tile([P, 2, N, 4], BF16, align_bytes=64)
+        identf = const.tile([P, P], F32)
+        make_identity(nc, identf[:])
+        uq = const.tile([P, 2, N * 4], BF16, align_bytes=64)
         ucodes = const.tile([P, 2, N], U32, align_bytes=64)
         uscales = const.tile([P, 2, N], U8, align_bytes=64)
+        gd = const.tile([P, 4096], BF16)
+        gdv = gd[:].rearrange("p (kw u x) -> p kw u x", kw=8, u=2)
 
-        xv = x[0].rearrange("c (s jl kh d) w -> jl (c s) kh (d w)", s=2, jl=16, kh=8, d=2)
-        attv = attentions[0, 0].rearrange("(h p r) j -> h p r j", h=NH, p=P, r=G)
-        ov = out[0].rearrange("c (h lh kh) (b w) -> c h b lh kh w", h=NH, kh=8, b=NB)
+        xv = x[0].rearrange("c (s r kh d) w -> r (c s) kh (d w)", s=2, r=16, kh=8, d=2)
+        attv = attentions[0, 0].rearrange("(p t) j -> p t j", p=P)
+        ov = out[0].rearrange("c (lh kh) (b z) -> b c lh kh z", kh=8, b=2)
 
-        xs = {}
-        chunks = {}
+        xs = []
+        rows = []
 
-        def load_x(k):
+        def load_x():
+            k = len(xs)
             xs_k = xpool.tile([P, 4, 2, 512], BF16, name="xs")
             for a in range(4):
-                nc.sync.dma_start(
-                    out=xs_k[:, a].rearrange("p d w -> p (d w)"), in_=xv[4 * k + a]
-                )
-            xs[k] = xs_k
+                nc.sync.dma_start(out=xs_k[:, a].rearrange("p d w -> p (d w)"), in_=xv[4 * k + a])
+            xs.append(xs_k)
 
-        def load_att(ci):
-            at_c = apool.tile([P, RC, LP], BF16, name="at_c")
-            h, r0 = divmod(ci * RC, G)
-            nc.sync.dma_start(out=at_c[:], in_=attv[h, :, r0 : r0 + RC, :])
-            chunks[ci] = at_c
+        def load_att(width):
+            at_c = apool.tile([P, 4, LP], BF16, name="at_c")
+            t0 = len(rows)
+            nc.sync.dma_start(out=at_c[:, 0:width, :], in_=attv[:, t0 : t0 + width, :])
+            for q in range(width):
+                rows.append(at_c[:, q, :])
 
-        for item in [["x",0],["a",0],["x",1],["a",1],["x",2],["x",3],["a",2],["a",3],["a",4],["a",5],["a",6],["a",7]]:
-            if item[0] == "x":
-                load_x(item[1])
+        nchunk = 0
+        for item in LOADS:
+            if item == "x":
+                load_x()
             else:
-                load_att(item[1])
-
-        def row(t):
-            return chunks[t // RC][:, t % RC, :]
+                load_att(CHUNKS[nchunk])
+                nchunk += 1
 
         state = {}
-
-        g = const.tile([P, 16 * 256], BF16)
 
         def pool_vector(k):
             s1 = const.tile([P, 4, 512], F32, name="s1")
             nc.vector.tensor_tensor(out=s1[:], in0=xs[k][:, :, 0, :], in1=xs[k][:, :, 1, :], op=ALU.add)
-            s1v = s1[:].rearrange("p a (m d) -> p (a m) d", d=2)
-            nc.vector.tensor_tensor(
-                out=g[:, k * 1024 : (k + 1) * 1024], in0=s1v[:, :, 0], in1=s1v[:, :, 1], op=ALU.add
-            )
+            for a in range(4):
+                r = 4 * k + a
+                sv = s1[:, a, :].rearrange("p (u f kw d) -> p d kw u f", u=2, f=16, kw=8, d=2)
+                nc.vector.tensor_tensor(
+                    out=gdv[:, :, :, r * 16 : (r + 1) * 16], in0=sv[:, 0], in1=sv[:, 1], op=ALU.add
+                )
 
         def pool_matmuls(k):
             banks = []
@@ -116,29 +115,29 @@ def tile_decode_atten_t_kernel(tc, x, attentions, out):
 
         def round_g(k):
             for beta in range(2):
-                c0 = (2 * k + beta) * 512
-                nc.scalar.copy(out=g[:, c0 : c0 + 512], in_=state[("ps", k)][beta][:])
+                pv = state[("ps", k)][beta][:].rearrange("p (a u f kw) -> p a kw u f", a=2, u=2, f=16, kw=8)
+                for a in range(2):
+                    r = 4 * k + 2 * beta + a
+                    nc.scalar.copy(out=gdv[:, :, :, r * 16 : (r + 1) * 16], in_=pv[:, a])
 
         def transpose_u(b):
-            tp = psum_o.tile([P, 1024], BF16, name="mo")
-            for kk in range(2):
-                for t in range(4):
-                    o = (4 * kk + t) * P
-                    nc.tensor.transpose(tp[:, o : o + P], g[:, t * 8 + 2 * b + kk :: 32], ident[:])
+            tp = psum_o.tile([P, 512], F32, name="mo")
+            words = gd[:].bitcast(F32)
+            for q in range(4):
+                w0 = (4 * b + q) * P
+                nc.tensor.transpose(tp[:, q * P : (q + 1) * P], words[:, w0 : w0 + P], identf[:])
             state[("tu", b)] = tp
 
         def regroup_u(b):
-            tv = state[("tu", b)][:].rearrange("p (q c s h) -> p s c h q", q=8, c=8, s=2, h=8)
+            tv = state[("tu", b)][:].rearrange("p (q c s h) -> p s c h q", q=4, c=8, s=2, h=8)
+            dst = uq[:].bitcast(F32).rearrange("p s (c h b q) -> p s b c h q", c=8, h=8, b=4, q=4)
             for s in range(2):
-                dst = uq[:, s].rearrange("p (c h b2 kk) t -> p b2 c h (kk t)", c=8, h=8, b2=4, kk=2)
-                nc.scalar.copy(out=dst[:, b], in_=tv[:, s])
+                nc.scalar.copy(out=dst[:, s, b], in_=tv[:, s])
 
         def quantise_u():
             for s in range(2):
                 nc.vector.quantize_mx(
-                    out=ucodes[:, s, :].bitcast(FP8X4),
-                    scales=uscales[:, s, :],
-                    in_=uq[:, s].rearrange("p n t -> p (n t)"),
+                    out=ucodes[:, s, :].bitcast(FP8X4), scales=uscales[:, s, :], in_=uq[:, s, :]
                 )
 
         def count(i):
@@ -147,7 +146,7 @@ def tile_decode_atten_t_kernel(tc, x, attentions, out):
                 junk = jpool.tile([P, LP], BF16, name="junk")
                 nc.vector.tensor_scalar(
                     out=junk[:],
-                    in0=row(2 * i + j),
+                    in0=rows[2 * i + j],
                     scalar1=0.0,
                     scalar2=1e-05,
                     op0=ALU.not_equal,
@@ -164,7 +163,11 @@ def tile_decode_atten_t_kernel(tc, x, attentions, out):
             for j in range(2):
                 a_t = work.tile([P, LP], BF16, name="a_t")
                 nc.vector.tensor_scalar(
-                    out=a_t[:], in0=row(2 * i + j), scalar1=rnz[:, j : j + 1], scalar2=None, op0=ALU.mult
+                    out=a_t[:].rearrange("p (u b f) -> p u b f", u=2, f=16),
+                    in0=rows[2 * i + j].rearrange("p (b u f) -> p u b f", u=2, f=16),
+                    scalar1=rnz[:, j : j + 1],
+                    scalar2=None,
+                    op0=ALU.mult,
                 )
                 tiles.append(a_t)
             state[("a", i)] = tiles
@@ -172,32 +175,29 @@ def tile_decode_atten_t_kernel(tc, x, attentions, out):
         def transpose(i):
             banks = []
             for j in range(2):
-                a_t = state[("a", i)][j]
-                tp = psum_t.tile([P, 1024], BF16, name="tp")
-                for b in range(8):
-                    nc.tensor.transpose(
-                        tp[:, b * P : (b + 1) * P], a_t[:, (b // 4) * 512 + b % 4 : (b // 4 + 1) * 512 : 4], ident[:]
-                    )
+                words = state[("a", i)][j][:].bitcast(F32)
+                tp = psum_t.tile([P, 512], F32, name="tp")
+                for b in range(4):
+                    nc.tensor.transpose(tp[:, b * P : (b + 1) * P], words[:, b * P : (b + 1) * P], identf[:])
                 banks.append(tp)
             state[("tp", i)] = banks
 
         def regroup(i):
-            grp = rpool.tile([P, 2, 2, P, 4], BF16, name="grp", align_bytes=64)
+            grp = rpool.tile([P, 2048], BF16, name="grp", align_bytes=64)
+            words = grp[:].bitcast(F32)
             for j in range(2):
                 nc.scalar.copy(
-                    out=grp[:, j], in_=state[("tp", i)][j][:].rearrange("p (s t l) -> p s l t", s=2, t=4)
+                    out=words[:, j * 512 : (j + 1) * 512].rearrange("p (s l u) -> p s l u", s=2, u=2),
+                    in_=state[("tp", i)][j][:].rearrange("p (u s l) -> p s l u", s=2, u=2),
                 )
             state[("grp", i)] = grp
 
         def quantise(i):
             codes = qpool.tile([P, 4 * P], U32, name="codes", align_bytes=64)
             scl = qpool.tile([P, 4 * P], U8, name="scl", align_bytes=64)
-            nc.vector.quantize_mx(
-                out=codes[:].bitcast(FP8X4),
-                scales=scl[:],
-                in_=state[("grp", i)][:].rearrange("p j s l t -> p (j s l t)"),
-            )
+            nc.vector.quantize_mx(out=codes[:].bitcast(FP8X4), scales=scl[:], in_=state[("grp", i)][:])
             state[("q", i)] = (codes, scl)
+
         def multiply(i):
             codes, scl = state[("q", i)]
             banks = []
@@ -217,73 +217,71 @@ def tile_decode_atten_t_kernel(tc, x, attentions, out):
                 banks.append(mo)
             state[("mo", i)] = banks
 
-
-        def store(h, stage, r0, r1):
-            for c in range(8):
-                for b in range(NB):
-                    nc.sync.dma_start(
-                        out=ov[c, h, b][:, :, r0 * 8 : r1 * 8],
-                        in_=stage[b:P:NB, c * 8 : (c + 1) * 8, r0:r1, :].rearrange("p kh r w -> p kh (r w)"),
-                    )
-
         def on_vector(t):
-            return t % 2 == 1
+            return t >= NT - 4 and t % 2 == 1
 
         def empty(i, vector):
             for j in range(2):
                 t = 2 * i + j
-                h, r = divmod(t, G)
+                h, r = divmod(t, HALF)
                 if ("stage", h) not in state:
-                    state[("stage", h)] = opool.tile([P, 64, G, 8], F32, name="stage")
-                stage = state[("stage", h)]
-                dst = stage[:, :, r, :]
+                    state[("stage", h)] = opool.tile([P, 64, HALF, 8], F32, name="stage")
+                dst = state[("stage", h)][:, :, r, :]
                 src = state[("mo", i)][j][:].rearrange("p (m w) -> p m w", w=8)
                 if vector and on_vector(t):
                     nc.vector.tensor_scalar(out=dst, in0=src, scalar1=0.25, scalar2=None, op0=ALU.mult)
                 if not vector and not on_vector(t):
                     nc.scalar.activation(out=dst, in_=src, func=ACT.Copy, scale=0.25)
 
-        def stores_after(i):
-            h, r = divmod(2 * i + 1, G)
+        def store(h, r0, r1):
             stage = state[("stage", h)]
-            if r == G // 2 - 1:
-                store(h, stage, 0, G // 2)
-            if r == G - 1:
-                store(h, stage, G // 2, G)
+            z0 = h * HALF * 8
+            for c in range(8):
+                for b in range(2):
+                    nc.sync.dma_start(
+                        out=ov[b, c][:, :, z0 + r0 * 8 : z0 + r1 * 8],
+                        in_=stage[b:P:2, c * 8 : (c + 1) * 8, r0:r1, :].rearrange("p kh r w -> p kh (r w)"),
+                    )
+
+        STORES = {7: (0, 0, 16), 11: (1, 0, 8), 15: (1, 8, 16)}
 
         def m_step(i):
-            return max(i + LM, M0 + (i + CR - 1) // CR)
+            return max(i + LM, M0 + (2 * i) // 3)
 
-        pool_vector(0)
         for n in range(NP + LM + 1):
             due = [i for i in range(NP) if m_step(i) == n]
+            last = [i for i in range(NP) if m_step(i) == n - 1]
+            for i in last:
+                empty(i, True)
+            if n < NP:
+                count(n)
             if n == UQ:
                 quantise_u()
-            for i in due:
-                multiply(i)
+            if 0 <= n - 2 < NP:
+                quantise(n - 2)
+            if n < NP:
+                scale(n)
+            if PX[0] == n:
+                pool_vector(0)
             for k in range(1, 4):
                 if PX[k] == n:
                     pool_matmuls(k)
-            if n == PX[3] + 1:
+            if n == TU:
                 for b in range(4):
                     transpose_u(b)
             if 0 <= n - 1 < NP:
                 transpose(n - 1)
             for i in due:
-                empty(i, True)
-            if n < NP:
-                count(n)
-                scale(n)
-            if 0 <= n - 2 < NP:
-                quantise(n - 2)
-            if n == PX[3] + 1:
-                for b in range(4):
-                    regroup_u(b)
-            for i in due:
+                multiply(i)
+            for i in last:
                 empty(i, False)
-                stores_after(i)
+                if i in STORES:
+                    store(*STORES[i])
             for k in range(1, 4):
                 if PX[k] == n:
                     round_g(k)
+            if n == TU:
+                for b in range(4):
+                    regroup_u(b)
             if 0 <= n - 1 < NP:
                 regroup(n - 1)

@@ -243,7 +243,7 @@ def tile_decode_atten_t_kernel(tc, x, attentions, out):
                         in_=stage[b:P:2, c * 8 : (c + 1) * 8, r0:r1, :].rearrange("p kh r w -> p kh (r w)"),
                     )
 
-        STORES = {7: (0, 0, 16), 11: (1, 0, 8), 15: (1, 8, 16)}
+        STORES = {7: (0, 0, 16), 15: (1, 0, 16)}
 
         def m_step(i):
             return max(i + LM, M0 + (2 * i) // 3)

@@ -20,12 +20,9 @@ FLOPS = 2 * L * LP * N
 NT = L // P
 NP = NT // 2
 HALF = NT // 2
-CHUNKS = [2, 2, 4, 4, 4, 4, 4, 4, 4]
-LOADS = ["a", "x", "a", "x", "x", "a", "x", "a", "a", "a", "a", "a", "a"]
-PX = [0, 1, 2, 4]
-TU = 5
-UQ = 6
-M0 = 6
+LOADS = "2xx2xxx2xxx2xxx2xxx2xx44444"
+U = 6
+POOL_STEP = [U - 3, U - 3, U - 2, U - 2, U - 1, U - 1]
 LM = 3
 
 
@@ -35,7 +32,9 @@ def tile_decode_atten_t_kernel(tc, x, attentions, out):
         ctx.enter_context(tc.manual_schedule())
         const = ctx.enter_context(tc.tile_pool(name="const", bufs=1))
         xpool = ctx.enter_context(tc.tile_pool(name="xpool", bufs=4))
-        apool = ctx.enter_context(tc.tile_pool(name="apool", bufs=7))
+        a2pool = ctx.enter_context(tc.tile_pool(name="a2pool", bufs=6))
+        a4pool = ctx.enter_context(tc.tile_pool(name="a4pool", bufs=5))
+        spool = ctx.enter_context(tc.tile_pool(name="spool", bufs=2))
         work = ctx.enter_context(tc.tile_pool(name="work", bufs=4))
         jpool = ctx.enter_context(tc.tile_pool(name="jpool", bufs=2))
         small = ctx.enter_context(tc.tile_pool(name="small", bufs=4))
@@ -60,65 +59,63 @@ def tile_decode_atten_t_kernel(tc, x, attentions, out):
         ov = out[0].rearrange("c (lh kh) (b z) -> b c lh kh z", kh=8, b=2)
 
         xs = []
+        xrows = []
         rows = []
 
         def load_x():
-            k = len(xs)
-            xs_k = xpool.tile([P, 4, 2, 512], BF16, name="xs")
-            for a in range(4):
-                nc.sync.dma_start(out=xs_k[:, a].rearrange("p d w -> p (d w)"), in_=xv[4 * k + a])
-            xs.append(xs_k)
+            k, a = divmod(len(xrows), 4)
+            if a == 0:
+                xs_k = xpool.tile([P, 4, 2, 512], BF16, name="xs")
+                xs.append(xs_k)
+            nc.sync.dma_start(out=xs[k][:, a].rearrange("p d w -> p (d w)"), in_=xv[4 * k + a])
+            xrows.append(xs[k][:, a])
 
         def load_att(width):
-            at_c = apool.tile([P, 4, LP], BF16, name="at_c")
+            if width == 2:
+                at_c = a2pool.tile([P, 2, LP], BF16, name="at_2")
+            else:
+                at_c = a4pool.tile([P, 4, LP], BF16, name="at_4")
             t0 = len(rows)
-            nc.sync.dma_start(out=at_c[:, 0:width, :], in_=attv[:, t0 : t0 + width, :])
+            nc.sync.dma_start(out=at_c[:], in_=attv[:, t0 : t0 + width, :])
             for q in range(width):
                 rows.append(at_c[:, q, :])
 
-        nchunk = 0
         for item in LOADS:
             if item == "x":
                 load_x()
             else:
-                load_att(CHUNKS[nchunk])
-                nchunk += 1
+                load_att(int(item))
 
         state = {}
 
-        def pool_vector(k):
-            s1 = const.tile([P, 4, 512], F32, name="s1")
-            nc.vector.tensor_tensor(out=s1[:], in0=xs[k][:, :, 0, :], in1=xs[k][:, :, 1, :], op=ALU.add)
-            for a in range(4):
-                r = 4 * k + a
-                sv = s1[:, a, :].rearrange("p (u f kw d) -> p d kw u f", u=2, f=16, kw=8, d=2)
-                nc.vector.tensor_tensor(
-                    out=gdv[:, :, :, r * 16 : (r + 1) * 16], in0=sv[:, 0], in1=sv[:, 1], op=ALU.add
-                )
+        def pool_gpsimd(r):
+            s1 = spool.tile([P, 512], F32, name="s1")
+            nc.gpsimd.tensor_tensor(out=s1[:], in0=xrows[r][:, 0, :], in1=xrows[r][:, 1, :], op=ALU.add)
+            sv = s1[:].rearrange("p (u f kw d) -> p d kw u f", u=2, f=16, kw=8, d=2)
+            nc.gpsimd.tensor_tensor(
+                out=gdv[:, :, :, r * 16 : (r + 1) * 16], in0=sv[:, 0], in1=sv[:, 1], op=ALU.add
+            )
 
-        def pool_matmuls(k):
-            banks = []
-            for beta in range(2):
-                ps = psum_o.tile([P, 512], F32, name="mo")
-                for d in range(2):
-                    cols = xs[k][:, 2 * beta : 2 * beta + 2, d, :].rearrange("p a (m e) -> p a m e", e=2)
-                    for e in range(2):
-                        nc.tensor.matmul(
-                            out=ps[:],
-                            lhsT=ident[:],
-                            rhs=cols[:, :, :, e],
-                            start=(d == 0 and e == 0),
-                            stop=(d == 1 and e == 1),
-                        )
-                banks.append(ps)
-            state[("ps", k)] = banks
+        def pool_matmuls(q):
+            ps = psum_o.tile([P, 512], F32, name="mo")
+            k, a = divmod(4 + 2 * q, 4)
+            for d in range(2):
+                cols = xs[k][:, a : a + 2, d, :].rearrange("p a (m e) -> p a m e", e=2)
+                for e in range(2):
+                    nc.tensor.matmul(
+                        out=ps[:],
+                        lhsT=ident[:],
+                        rhs=cols[:, :, :, e],
+                        start=(d == 0 and e == 0),
+                        stop=(d == 1 and e == 1),
+                    )
+            state[("ps", q)] = ps
 
-        def round_g(k):
-            for beta in range(2):
-                pv = state[("ps", k)][beta][:].rearrange("p (a u f kw) -> p a kw u f", a=2, u=2, f=16, kw=8)
-                for a in range(2):
-                    r = 4 * k + 2 * beta + a
-                    nc.scalar.copy(out=gdv[:, :, :, r * 16 : (r + 1) * 16], in_=pv[:, a])
+        def round_g(q):
+            pv = state[("ps", q)][:].rearrange("p (a u f kw) -> p a kw u f", a=2, u=2, f=16, kw=8)
+            for a in range(2):
+                r = 4 + 2 * q + a
+                nc.scalar.copy(out=gdv[:, :, :, r * 16 : (r + 1) * 16], in_=pv[:, a])
 
         def transpose_u(b):
             tp = psum_o.tile([P, 512], F32, name="mo")
@@ -142,6 +139,7 @@ def tile_decode_atten_t_kernel(tc, x, attentions, out):
 
         def count(i):
             nz = small.tile([P, 2], F32, name="nz")
+            state[("nz", i)] = nz
             for j in range(2):
                 junk = jpool.tile([P, LP], BF16, name="junk")
                 nc.vector.tensor_scalar(
@@ -153,8 +151,10 @@ def tile_decode_atten_t_kernel(tc, x, attentions, out):
                     op1=ALU.add,
                     accum_out=nz[:, j : j + 1],
                 )
+
+        def invert(i):
             rnz = small.tile([P, 2], F32, name="rnz")
-            nc.vector.reciprocal(out=rnz[:], in_=nz[:])
+            nc.vector.reciprocal(out=rnz[:], in_=state[("nz", i)][:])
             state[("rnz", i)] = rnz
 
         def scale(i):
@@ -218,7 +218,7 @@ def tile_decode_atten_t_kernel(tc, x, attentions, out):
             state[("mo", i)] = banks
 
         def on_vector(t):
-            return t >= NT - 4 and t % 2 == 1
+            return t % 8 == 3 or (t >= NT - 6 and t % 2 == 1)
 
         def empty(i, vector):
             for j in range(2):
@@ -246,41 +246,43 @@ def tile_decode_atten_t_kernel(tc, x, attentions, out):
         STORES = {7: (0, 0, 16), 15: (1, 0, 16)}
 
         def m_step(i):
-            return max(i + LM, M0 + (2 * i) // 3)
+            return max(i + LM, U + 1 + (2 * i) // 3)
 
-        for n in range(NP + LM + 1):
+        for r in range(4):
+            pool_gpsimd(r)
+        for n in range(m_step(NP - 1) + 2):
             due = [i for i in range(NP) if m_step(i) == n]
             last = [i for i in range(NP) if m_step(i) == n - 1]
+            if n == U + 1:
+                quantise_u()
+            if n < NP:
+                count(n)
             for i in last:
                 empty(i, True)
             if n < NP:
-                count(n)
-            if n == UQ:
-                quantise_u()
+                invert(n)
             if 0 <= n - 2 < NP:
                 quantise(n - 2)
             if n < NP:
                 scale(n)
-            if PX[0] == n:
-                pool_vector(0)
-            for k in range(1, 4):
-                if PX[k] == n:
-                    pool_matmuls(k)
-            if n == TU:
-                for b in range(4):
-                    transpose_u(b)
             if 0 <= n - 1 < NP:
                 transpose(n - 1)
+            for q in range(6):
+                if POOL_STEP[q] == n:
+                    pool_matmuls(q)
+            if n == U:
+                for b in range(4):
+                    transpose_u(b)
             for i in due:
                 multiply(i)
             for i in last:
                 empty(i, False)
                 if i in STORES:
                     store(*STORES[i])
-            for k in range(1, 4):
-                if PX[k] == n:
-                    round_g(k)
-            if n == TU:
+            for q in range(6):
+                if POOL_STEP[q] == n:
+                    round_g(q)
+            if n == U:
                 for b in range(4):
                     regroup_u(b)
             if 0 <= n - 1 < NP:

@@ -19,11 +19,11 @@ FLOPS = 2 * L * LP * N
 
 NT = L // P
 NP = NT // 2
-HALF = NT // 2
 LOADS = "2xx2xxx2xxx2xxx2xxx2xx44444"
 U = 6
 POOL_STEP = [U - 3, U - 3, U - 2, U - 2, U - 1, U - 1]
 LM = 3
+GROUPS = [0, 8, 20]
 
 
 def tile_decode_atten_t_kernel(tc, x, attentions, out):
@@ -40,7 +40,7 @@ def tile_decode_atten_t_kernel(tc, x, attentions, out):
         small = ctx.enter_context(tc.tile_pool(name="small", bufs=4))
         rpool = ctx.enter_context(tc.tile_pool(name="rpool", bufs=3))
         qpool = ctx.enter_context(tc.tile_pool(name="qpool", bufs=8))
-        opool = ctx.enter_context(tc.tile_pool(name="opool", bufs=2))
+        opool = ctx.enter_context(tc.tile_pool(name="opool", bufs=1))
         psum_t = ctx.enter_context(tc.psum_pool(name="psum_t", bufs=4))
         psum_o = ctx.enter_context(tc.psum_pool(name="psum_o", bufs=4))
 
@@ -54,7 +54,7 @@ def tile_decode_atten_t_kernel(tc, x, attentions, out):
         gd = const.tile([P, 4096], BF16)
         gdv = gd[:].rearrange("p (kw u x) -> p kw u x", kw=8, u=2)
 
-        xv = x[0].rearrange("c (s r kh d) w -> r (c s) kh (d w)", s=2, r=16, kh=8, d=2)
+        xv = x[0].rearrange("c (r s kh d) w -> r (s kh) c (d w)", s=2, r=16, kh=8, d=2)
         attv = attentions[0, 0].rearrange("(p t) j -> p t j", p=P)
         ov = out[0].rearrange("c (lh kh) (b z) -> b c lh kh z", kh=8, b=2)
 
@@ -126,7 +126,7 @@ def tile_decode_atten_t_kernel(tc, x, attentions, out):
             state[("tu", b)] = tp
 
         def regroup_u(b):
-            tv = state[("tu", b)][:].rearrange("p (q c s h) -> p s c h q", q=4, c=8, s=2, h=8)
+            tv = state[("tu", b)][:].rearrange("p (q s h c) -> p s c h q", q=4, c=8, s=2, h=8)
             dst = uq[:].bitcast(F32).rearrange("p s (c h b q) -> p s b c h q", c=8, h=8, b=4, q=4)
             for s in range(2):
                 nc.scalar.copy(out=dst[:, s, b], in_=tv[:, s])
@@ -163,8 +163,8 @@ def tile_decode_atten_t_kernel(tc, x, attentions, out):
             for j in range(2):
                 a_t = work.tile([P, LP], BF16, name="a_t")
                 nc.vector.tensor_scalar(
-                    out=a_t[:].rearrange("p (u b f) -> p u b f", u=2, f=16),
-                    in0=rows[2 * i + j].rearrange("p (b u f) -> p u b f", u=2, f=16),
+                    out=a_t[:].rearrange("p (v r f) -> p v r f", v=4, f=16),
+                    in0=rows[2 * i + j].rearrange("p (r v f) -> p v r f", v=4, f=16),
                     scalar1=rnz[:, j : j + 1],
                     scalar2=None,
                     op0=ALU.mult,
@@ -188,7 +188,7 @@ def tile_decode_atten_t_kernel(tc, x, attentions, out):
             for j in range(2):
                 nc.scalar.copy(
                     out=words[:, j * 512 : (j + 1) * 512].rearrange("p (s l u) -> p s l u", s=2, u=2),
-                    in_=state[("tp", i)][j][:].rearrange("p (u s l) -> p s l u", s=2, u=2),
+                    in_=state[("tp", i)][j][:].rearrange("p (s u l) -> p s l u", s=2, u=2),
                 )
             state[("grp", i)] = grp
 
@@ -217,36 +217,35 @@ def tile_decode_atten_t_kernel(tc, x, attentions, out):
                 banks.append(mo)
             state[("mo", i)] = banks
 
+        stages = {}
+        ends = GROUPS[1:] + [NT]
+
         def on_vector(t):
             return t % 8 == 3 or (t >= NT - 6 and t % 2 == 1)
 
         def empty(i, vector):
             for j in range(2):
                 t = 2 * i + j
-                h, r = divmod(t, HALF)
-                if ("stage", h) not in state:
-                    state[("stage", h)] = opool.tile([P, 64, HALF, 8], F32, name="stage")
-                dst = state[("stage", h)][:, :, r, :]
+                h = max(g for g in range(len(GROUPS)) if GROUPS[g] <= t)
+                if h not in stages:
+                    stages[h] = opool.tile([P, 64, ends[h] - GROUPS[h], 8], F32, name="stage%d" % h)
+                dst = stages[h][:, :, t - GROUPS[h], :]
                 src = state[("mo", i)][j][:].rearrange("p (m w) -> p m w", w=8)
                 if vector and on_vector(t):
                     nc.vector.tensor_scalar(out=dst, in0=src, scalar1=0.25, scalar2=None, op0=ALU.mult)
                 if not vector and not on_vector(t):
                     nc.scalar.activation(out=dst, in_=src, func=ACT.Copy, scale=0.25)
 
-        def store(h, r0, r1):
-            stage = state[("stage", h)]
-            z0 = h * HALF * 8
+        def store(h):
             for c in range(8):
                 for b in range(2):
                     nc.sync.dma_start(
-                        out=ov[b, c][:, :, z0 + r0 * 8 : z0 + r1 * 8],
-                        in_=stage[b:P:2, c * 8 : (c + 1) * 8, r0:r1, :].rearrange("p kh r w -> p kh (r w)"),
+                        out=ov[b, c][:, :, GROUPS[h] * 8 : ends[h] * 8],
+                        in_=stages[h][b:P:2, c * 8 : (c + 1) * 8, :, :].rearrange("p kh r w -> p kh (r w)"),
                     )
 
-        STORES = {7: (0, 0, 16), 15: (1, 0, 16)}
-
         def m_step(i):
-            return max(i + LM, U + 1 + (2 * i) // 3)
+            return max(i + LM, U + 1 + i // 2)
 
         for r in range(4):
             pool_gpsimd(r)
@@ -277,8 +276,8 @@ def tile_decode_atten_t_kernel(tc, x, attentions, out):
                 multiply(i)
             for i in last:
                 empty(i, False)
-                if i in STORES:
-                    store(*STORES[i])
+                if 2 * i + 2 in ends:
+                    store(ends.index(2 * i + 2))
             for q in range(6):
                 if POOL_STEP[q] == n:
                     round_g(q)

from contextlib import ExitStack

import concourse.mybir as mybir
from concourse.masks import make_identity

BF16 = mybir.dt.bfloat16
F32 = mybir.dt.float32
U32 = mybir.dt.uint32
U8 = mybir.dt.uint8
FP8X4 = mybir.dt.float8_e4m3fn_x4
ALU = mybir.AluOpType
ACT = mybir.ActivationFunctionType

P = 128
L = 4096
LP = 1024
N = 512
FLOPS = 2 * L * LP * N

NT = L // P
NP = NT // 2
LOADS = "2xx2xxx2xxx2xxx2xxx2xx44444"
U = 6
POOL_STEP = [U - 3, U - 3, U - 2, U - 2, U - 1, U - 1]
LM = 3
GROUPS = [0, 8, 20]


def tile_decode_atten_t_kernel(tc, x, attentions, out):
    nc = tc.nc
    with ExitStack() as ctx:
        ctx.enter_context(tc.manual_schedule())
        const = ctx.enter_context(tc.tile_pool(name="const", bufs=1))
        xpool = ctx.enter_context(tc.tile_pool(name="xpool", bufs=4))
        a2pool = ctx.enter_context(tc.tile_pool(name="a2pool", bufs=6))
        a4pool = ctx.enter_context(tc.tile_pool(name="a4pool", bufs=5))
        spool = ctx.enter_context(tc.tile_pool(name="spool", bufs=2))
        work = ctx.enter_context(tc.tile_pool(name="work", bufs=4))
        jpool = ctx.enter_context(tc.tile_pool(name="jpool", bufs=2))
        small = ctx.enter_context(tc.tile_pool(name="small", bufs=4))
        rpool = ctx.enter_context(tc.tile_pool(name="rpool", bufs=3))
        qpool = ctx.enter_context(tc.tile_pool(name="qpool", bufs=8))
        opool = ctx.enter_context(tc.tile_pool(name="opool", bufs=1))
        psum_t = ctx.enter_context(tc.psum_pool(name="psum_t", bufs=4))
        psum_o = ctx.enter_context(tc.psum_pool(name="psum_o", bufs=4))

        ident = const.tile([P, P], BF16)
        make_identity(nc, ident[:])
        identf = const.tile([P, P], F32)
        make_identity(nc, identf[:])
        uq = const.tile([P, 2, N * 4], BF16, align_bytes=64)
        ucodes = const.tile([P, 2, N], U32, align_bytes=64)
        uscales = const.tile([P, 2, N], U8, align_bytes=64)
        gd = const.tile([P, 4096], BF16)
        gdv = gd[:].rearrange("p (kw u x) -> p kw u x", kw=8, u=2)

        xv = x[0].rearrange("c (r s kh d) w -> r (s kh) c (d w)", s=2, r=16, kh=8, d=2)
        attv = attentions[0, 0].rearrange("(p t) j -> p t j", p=P)
        ov = out[0].rearrange("c (lh kh) (b z) -> b c lh kh z", kh=8, b=2)

        xs = []
        xrows = []
        rows = []

        def load_x():
            k, a = divmod(len(xrows), 4)
            if a == 0:
                xs_k = xpool.tile([P, 4, 2, 512], BF16, name="xs")
                xs.append(xs_k)
            nc.sync.dma_start(out=xs[k][:, a].rearrange("p d w -> p (d w)"), in_=xv[4 * k + a])
            xrows.append(xs[k][:, a])

        def load_att(width):
            if width == 2:
                at_c = a2pool.tile([P, 2, LP], BF16, name="at_2")
            else:
                at_c = a4pool.tile([P, 4, LP], BF16, name="at_4")
            t0 = len(rows)
            nc.sync.dma_start(out=at_c[:], in_=attv[:, t0 : t0 + width, :])
            for q in range(width):
                rows.append(at_c[:, q, :])

        for item in LOADS:
            if item == "x":
                load_x()
            else:
                load_att(int(item))

        state = {}

        def pool_gpsimd(r):
            s1 = spool.tile([P, 512], F32, name="s1")
            nc.gpsimd.tensor_tensor(out=s1[:], in0=xrows[r][:, 0, :], in1=xrows[r][:, 1, :], op=ALU.add)
            sv = s1[:].rearrange("p (u f kw d) -> p d kw u f", u=2, f=16, kw=8, d=2)
            nc.gpsimd.tensor_tensor(
                out=gdv[:, :, :, r * 16 : (r + 1) * 16], in0=sv[:, 0], in1=sv[:, 1], op=ALU.add
            )

        def pool_matmuls(q):
            ps = psum_o.tile([P, 512], F32, name="mo")
            k, a = divmod(4 + 2 * q, 4)
            for d in range(2):
                cols = xs[k][:, a : a + 2, d, :].rearrange("p a (m e) -> p a m e", e=2)
                for e in range(2):
                    nc.tensor.matmul(
                        out=ps[:],
                        lhsT=ident[:],
                        rhs=cols[:, :, :, e],
                        start=(d == 0 and e == 0),
                        stop=(d == 1 and e == 1),
                    )
            state[("ps", q)] = ps

        def round_g(q):
            pv = state[("ps", q)][:].rearrange("p (a u f kw) -> p a kw u f", a=2, u=2, f=16, kw=8)
            for a in range(2):
                r = 4 + 2 * q + a
                nc.scalar.copy(out=gdv[:, :, :, r * 16 : (r + 1) * 16], in_=pv[:, a])

        def transpose_u(b):
            tp = psum_o.tile([P, 512], F32, name="mo")
            words = gd[:].bitcast(F32)
            for q in range(4):
                w0 = (4 * b + q) * P
                nc.tensor.transpose(tp[:, q * P : (q + 1) * P], words[:, w0 : w0 + P], identf[:])
            state[("tu", b)] = tp

        def regroup_u(b):
            tv = state[("tu", b)][:].rearrange("p (q s h c) -> p s c h q", q=4, c=8, s=2, h=8)
            dst = uq[:].bitcast(F32).rearrange("p s (c h b q) -> p s b c h q", c=8, h=8, b=4, q=4)
            for s in range(2):
                nc.scalar.copy(out=dst[:, s, b], in_=tv[:, s])

        def quantise_u():
            for s in range(2):
                nc.vector.quantize_mx(
                    out=ucodes[:, s, :].bitcast(FP8X4), scales=uscales[:, s, :], in_=uq[:, s, :]
                )

        def count(i):
            nz = small.tile([P, 2], F32, name="nz")
            state[("nz", i)] = nz
            for j in range(2):
                junk = jpool.tile([P, LP], BF16, name="junk")
                nc.vector.tensor_scalar(
                    out=junk[:],
                    in0=rows[2 * i + j],
                    scalar1=0.0,
                    scalar2=1e-05,
                    op0=ALU.not_equal,
                    op1=ALU.add,
                    accum_out=nz[:, j : j + 1],
                )

        def invert(i):
            rnz = small.tile([P, 2], F32, name="rnz")
            nc.vector.reciprocal(out=rnz[:], in_=state[("nz", i)][:])
            state[("rnz", i)] = rnz

        def scale(i):
            rnz = state[("rnz", i)]
            tiles = []
            for j in range(2):
                a_t = work.tile([P, LP], BF16, name="a_t")
                nc.vector.tensor_scalar(
                    out=a_t[:].rearrange("p (v r f) -> p v r f", v=4, f=16),
                    in0=rows[2 * i + j].rearrange("p (r v f) -> p v r f", v=4, f=16),
                    scalar1=rnz[:, j : j + 1],
                    scalar2=None,
                    op0=ALU.mult,
                )
                tiles.append(a_t)
            state[("a", i)] = tiles

        def transpose(i):
            banks = []
            for j in range(2):
                words = state[("a", i)][j][:].bitcast(F32)
                tp = psum_t.tile([P, 512], F32, name="tp")
                for b in range(4):
                    nc.tensor.transpose(tp[:, b * P : (b + 1) * P], words[:, b * P : (b + 1) * P], identf[:])
                banks.append(tp)
            state[("tp", i)] = banks

        def regroup(i):
            grp = rpool.tile([P, 2048], BF16, name="grp", align_bytes=64)
            words = grp[:].bitcast(F32)
            for j in range(2):
                nc.scalar.copy(
                    out=words[:, j * 512 : (j + 1) * 512].rearrange("p (s l u) -> p s l u", s=2, u=2),
                    in_=state[("tp", i)][j][:].rearrange("p (s u l) -> p s l u", s=2, u=2),
                )
            state[("grp", i)] = grp

        def quantise(i):
            codes = qpool.tile([P, 4 * P], U32, name="codes", align_bytes=64)
            scl = qpool.tile([P, 4 * P], U8, name="scl", align_bytes=64)
            nc.vector.quantize_mx(out=codes[:].bitcast(FP8X4), scales=scl[:], in_=state[("grp", i)][:])
            state[("q", i)] = (codes, scl)

        def multiply(i):
            codes, scl = state[("q", i)]
            banks = []
            for j in range(2):
                mo = psum_o.tile([P, N], F32, name="mo")
                for s in range(2):
                    c0 = (2 * j + s) * P
                    nc.tensor.matmul_mx(
                        out=mo[:],
                        lhsT=codes[:, c0 : c0 + P].bitcast(FP8X4),
                        lhsT_scale=scl[:, c0 : c0 + P],
                        rhs=ucodes[:, s, :].bitcast(FP8X4),
                        rhs_scale=uscales[:, s, :],
                        start=(s == 0),
                        stop=(s == 1),
                    )
                banks.append(mo)
            state[("mo", i)] = banks

        stages = {}
        ends = GROUPS[1:] + [NT]

        def on_vector(t):
            return t % 8 == 3 or (t >= NT - 6 and t % 2 == 1)

        def empty(i, vector):
            for j in range(2):
                t = 2 * i + j
                h = max(g for g in range(len(GROUPS)) if GROUPS[g] <= t)
                if h not in stages:
                    stages[h] = opool.tile([P, 64, ends[h] - GROUPS[h], 8], F32, name="stage%d" % h)
                dst = stages[h][:, :, t - GROUPS[h], :]
                src = state[("mo", i)][j][:].rearrange("p (m w) -> p m w", w=8)
                if vector and on_vector(t):
                    nc.vector.tensor_scalar(out=dst, in0=src, scalar1=0.25, scalar2=None, op0=ALU.mult)
                if not vector and not on_vector(t):
                    nc.scalar.activation(out=dst, in_=src, func=ACT.Copy, scale=0.25)

        def store(h):
            for c in range(8):
                for b in range(2):
                    nc.sync.dma_start(
                        out=ov[b, c][:, :, GROUPS[h] * 8 : ends[h] * 8],
                        in_=stages[h][b:P:2, c * 8 : (c + 1) * 8, :, :].rearrange("p kh r w -> p kh (r w)"),
                    )

        def m_step(i):
            return max(i + LM, U + 1 + i // 2)

        for r in range(4):
            pool_gpsimd(r)
        for n in range(m_step(NP - 1) + 2):
            due = [i for i in range(NP) if m_step(i) == n]
            last = [i for i in range(NP) if m_step(i) == n - 1]
            if n == U + 1:
                quantise_u()
            if n < NP:
                count(n)
            for i in last:
                empty(i, True)
            if n < NP:
                invert(n)
            if 0 <= n - 2 < NP:
                quantise(n - 2)
            if n < NP:
                scale(n)
            if 0 <= n - 1 < NP:
                transpose(n - 1)
            for q in range(6):
                if POOL_STEP[q] == n:
                    pool_matmuls(q)
            if n == U:
                for b in range(4):
                    transpose_u(b)
            for i in due:
                multiply(i)
            for i in last:
                empty(i, False)
                if 2 * i + 2 in ends:
                    store(ends.index(2 * i + 2))
            for q in range(6):
                if POOL_STEP[q] == n:
                    round_g(q)
            if n == U:
                for b in range(4):
                    regroup_u(b)
            if 0 <= n - 1 < NP:
                regroup(n - 1)
